import numpy as np
import ml_dtypes

BF16 = ml_dtypes.bfloat16


def bf(x):
    return np.asarray(x, np.float32).astype(BF16)


def f32(x):
    return np.asarray(x, np.float32)


def f64(x):
    return np.asarray(x).astype(np.float64)


def striped(idx):
    return np.tile(idx.reshape(-1, 16).T, (8, 1))


B, Q, R, D, E, O, M, V, N, AL = 8, 16, 128, 256, 128, 128, 256, 4096, 2048, 3


def position_weights(start):
    pos = np.arange(Q)[None, :]
    st = start[:, None]
    en = st + AL - 1
    return np.where(pos < st, 1.0 - (st - pos) / Q, np.where(pos > en, 1.0 - (pos - en) / Q, 0.0))


def setup_inputs():
    table = bf(np.random.standard_normal((V, E)))
    w = bf(np.random.standard_normal((E, M)) / np.sqrt(E))
    h = bf(np.random.standard_normal((D, R)))
    wh = bf(np.random.standard_normal((D, M)) / np.sqrt(D))
    posw = f32(position_weights(np.random.permutation(Q - AL)[:B]).reshape(1, R))
    b = f32(0.1 * np.random.standard_normal((M, 1)))
    return {"table": table, "w": w, "h": h, "wh": wh, "posw": posw, "b": b, "offs": striped(np.random.permutation(V)[:N])}


def reference(table, w, h, wh, posw, b, offs):
    idx = offs[:16].T.reshape(-1)
    edge = f64(w).T @ f64(table)[idx].T
    node = f64(posw) * (f64(wh).T @ f64(h)) + f64(b)
    p = edge + np.repeat(node, Q, axis=1)
    return p[:O] * p[O:]

@@ -1,0 +1,101 @@
+import concourse.masks as masks
+import concourse.mybir as mybir
+
+BF16, F32, U16 = mybir.dt.bfloat16, mybir.dt.float32, mybir.dt.uint16
+ADD, MULT = mybir.AluOpType.add, mybir.AluOpType.mult
+
+P = 128
+V = 4096
+N = 2048
+Q = 16
+D = 256
+M = 256
+HALVES = M // P
+PIECE = 512
+WORDS = PIECE // Q
+BLOCKS = 4
+
+FLOPS = 2 * P * M * N + 2 * D * M * P
+
+
+def tile_typeenhancedgcndeepseek_kernel(tc, table, w, h, wh, posw, b, offs, out):
+    nc = tc.nc
+    with (
+        tc.tile_pool(name="held", bufs=1) as held,
+        tc.tile_pool(name="rows", bufs=V // (BLOCKS * P)) as rows,
+        tc.tile_pool(name="work", bufs=2) as work,
+        tc.psum_pool(name="flip", bufs=2) as flip,
+        tc.psum_pool(name="proj", bufs=2) as proj,
+        tc.psum_pool(name="pair", bufs=2) as pair,
+    ):
+        offsets = held.tile([P, N // 16], U16, name="offsets")
+        nc.sync.dma_start(offsets[:], offs)
+
+        identity = held.tile([P, P], BF16, name="identity")
+        masks.make_identity(nc, identity[:])
+
+        window = held.tile([P, V], BF16, name="window")
+        table_blocks = table.rearrange("(c p) e -> p c e", p=P)
+        for g in range(V // (BLOCKS * P)):
+            loaded = rows.tile([P, BLOCKS, P], BF16, name="loaded")
+            queue = nc.sync if g % 2 == 0 else nc.scalar
+            queue.dma_start(loaded[:], table_blocks[:, g * BLOCKS : (g + 1) * BLOCKS, :])
+            turned = flip.tile([P, BLOCKS * P], BF16, name="turned")
+            for i in range(BLOCKS):
+                nc.tensor.transpose(turned[:, i * P : (i + 1) * P], loaded[:, i, :], identity[:])
+            columns = window[:, g * BLOCKS * P : (g + 1) * BLOCKS * P]
+            if g % 2 == 0:
+                nc.vector.tensor_copy(columns, turned[:])
+            else:
+                nc.scalar.copy(columns, turned[:])
+
+        w_sb = held.tile([P, M], BF16, name="w_sb")
+        nc.gpsimd.dma_start(w_sb[:], w)
+        wh_sb = held.tile([P, D // P, M], BF16, name="wh_sb")
+        nc.gpsimd.dma_start(wh_sb[:], wh.rearrange("(k p) m -> p k m", p=P))
+        h_sb = held.tile([P, D // P, P], BF16, name="h_sb")
+        nc.gpsimd.dma_start(h_sb[:], h.rearrange("(k p) r -> p k r", p=P))
+        posw_all = held.tile([P, P], F32, name="posw_all")
+        nc.gpsimd.dma_start(posw_all[:], posw.rearrange("o r -> (o r)").partition_broadcast(P))
+
+        node = []
+        for t in range(HALVES):
+            bias = held.tile([P, 1], F32, name=f"bias{t}")
+            nc.gpsimd.dma_start(bias[:], b[t * P : (t + 1) * P, :])
+            word_proj = proj.tile([P, P], F32, name="word_proj")
+            for k in range(D // P):
+                nc.tensor.matmul(
+                    word_proj[:], wh_sb[:, k, t * P : (t + 1) * P], h_sb[:, k, :],
+                    start=(k == 0), stop=(k == D // P - 1),
+                )
+            weighted = work.tile([P, P], F32, name="weighted")
+            nc.vector.tensor_tensor(weighted[:], word_proj[:], posw_all[:], MULT)
+            node_t = held.tile([P, P], F32, name=f"node{t}")
+            nc.vector.tensor_scalar_add(node_t[:], weighted[:], bias[:])
+            node.append(node_t)
+
+        for piece in range(N // PIECE):
+            piece_offsets = offsets[:, piece * (PIECE // 16) : (piece + 1) * (PIECE // 16)]
+            summed = []
+            for t in range(HALVES):
+                edge = pair.tile([P, PIECE], F32, name=f"edge{t}")
+                nc.tensor.matmul(
+                    edge[:], w_sb[:, t * P : (t + 1) * P], window[:].indirect(piece_offsets),
+                    start=True, stop=True,
+                )
+                p_t = work.tile([P, PIECE], F32, name=f"p{t}")
+                node_of_pair = (
+                    node[t][:, piece * WORDS : (piece + 1) * WORDS]
+                    .unsqueeze(2)
+                    .to_broadcast([P, WORDS, Q])
+                )
+                nc.vector.tensor_tensor(
+                    p_t[:].rearrange("m (r q) -> m r q", q=Q),
+                    edge[:].rearrange("m (r q) -> m r q", q=Q),
+                    node_of_pair,
+                    ADD,
+                )
+                summed.append(p_t)
+            product = work.tile([P, PIECE], F32, name="product")
+            nc.vector.tensor_tensor(product[:], summed[0][:], summed[1][:], MULT)
+            nc.sync.dma_start(out[:, piece * PIECE : (piece + 1) * PIECE], product[:])

@@ -23,13 +23,16 @@ def tile_typeenhancedgcndeepseek_kernel(tc, table, w, h, wh, posw, b, offs, out)
     with (
         tc.tile_pool(name="held", bufs=1) as held,
         tc.tile_pool(name="rows", bufs=V // (BLOCKS * P)) as rows,
-        tc.tile_pool(name="work", bufs=2) as work,
+        tc.tile_pool(name="work", bufs=N // PIECE) as work,
         tc.psum_pool(name="flip", bufs=2) as flip,
         tc.psum_pool(name="proj", bufs=2) as proj,
         tc.psum_pool(name="pair", bufs=2) as pair,
     ):
         offsets = held.tile([P, N // 16], U16, name="offsets")
         nc.sync.dma_start(offsets[:], offs)
+
+        w_sb = held.tile([P, M], BF16, name="w_sb")
+        nc.scalar.dma_start(w_sb[:], w)
 
         identity = held.tile([P, P], BF16, name="identity")
         masks.make_identity(nc, identity[:])
@@ -49,19 +52,17 @@ def tile_typeenhancedgcndeepseek_kernel(tc, table, w, h, wh, posw, b, offs, out)
             else:
                 nc.scalar.copy(columns, turned[:])
 
-        w_sb = held.tile([P, M], BF16, name="w_sb")
-        nc.gpsimd.dma_start(w_sb[:], w)
         wh_sb = held.tile([P, D // P, M], BF16, name="wh_sb")
-        nc.gpsimd.dma_start(wh_sb[:], wh.rearrange("(k p) m -> p k m", p=P))
+        nc.sync.dma_start(wh_sb[:], wh.rearrange("(k p) m -> p k m", p=P))
         h_sb = held.tile([P, D // P, P], BF16, name="h_sb")
-        nc.gpsimd.dma_start(h_sb[:], h.rearrange("(k p) r -> p k r", p=P))
+        nc.scalar.dma_start(h_sb[:], h.rearrange("(k p) r -> p k r", p=P))
         posw_all = held.tile([P, P], F32, name="posw_all")
-        nc.gpsimd.dma_start(posw_all[:], posw.rearrange("o r -> (o r)").partition_broadcast(P))
+        nc.sync.dma_start(posw_all[:], posw.rearrange("o r -> (o r)").partition_broadcast(P))
 
         node = []
         for t in range(HALVES):
             bias = held.tile([P, 1], F32, name=f"bias{t}")
-            nc.gpsimd.dma_start(bias[:], b[t * P : (t + 1) * P, :])
+            nc.scalar.dma_start(bias[:], b[t * P : (t + 1) * P, :])
             word_proj = proj.tile([P, P], F32, name="word_proj")
             for k in range(D // P):
                 nc.tensor.matmul(
@@ -97,5 +98,6 @@ def tile_typeenhancedgcndeepseek_kernel(tc, table, w, h, wh, posw, b, offs, out)
                 )
                 summed.append(p_t)
             product = work.tile([P, PIECE], F32, name="product")
-            nc.vector.tensor_tensor(product[:], summed[0][:], summed[1][:], MULT)
+            multiplier = nc.gpsimd if piece < N // PIECE - 1 else nc.vector
+            multiplier.tensor_tensor(product[:], summed[0][:], summed[1][:], MULT)
             nc.sync.dma_start(out[:, piece * PIECE : (piece + 1) * PIECE], product[:])

@@ -20,50 +20,43 @@ FLOPS = 2 * P * M * N + 2 * D * M * P
 
 def tile_typeenhancedgcndeepseek_kernel(tc, table, w, h, wh, posw, b, offs, out):
     nc = tc.nc
+    load_rows = BLOCKS * P
+    loads = V // load_rows
     with (
         tc.tile_pool(name="held", bufs=1) as held,
-        tc.tile_pool(name="rows", bufs=V // (BLOCKS * P)) as rows,
+        tc.tile_pool(name="rows", bufs=loads) as rows,
         tc.tile_pool(name="work", bufs=N // PIECE) as work,
-        tc.psum_pool(name="flip", bufs=2) as flip,
-        tc.psum_pool(name="proj", bufs=2) as proj,
-        tc.psum_pool(name="pair", bufs=2) as pair,
+        tc.psum_pool(name="banks", bufs=8) as banks,
     ):
-        offsets = held.tile([P, N // 16], U16, name="offsets")
-        nc.sync.dma_start(offsets[:], offs)
-
-        w_sb = held.tile([P, M], BF16, name="w_sb")
-        nc.scalar.dma_start(w_sb[:], w)
+        h_sb = held.tile([P, D // P, P], BF16, name="h_sb")
+        nc.sync.dma_start(h_sb[:], h.rearrange("(k p) r -> p k r", p=P))
+        wh_sb = held.tile([P, D // P, M], BF16, name="wh_sb")
+        nc.scalar.dma_start(wh_sb[:], wh.rearrange("(k p) m -> p k m", p=P))
+        posw_all = held.tile([P, P], F32, name="posw_all")
+        nc.sync.dma_start(posw_all[:], posw.rearrange("o r -> (o r)").partition_broadcast(P))
+        bias = held.tile([P, HALVES], F32, name="bias")
+        with nc.allow_non_contiguous_dma(reason="256 single elements, one to a partition and layer"):
+            nc.scalar.dma_start(bias[:], b.rearrange("(t p) o -> p (t o)", p=P))
 
         identity = held.tile([P, P], BF16, name="identity")
         masks.make_identity(nc, identity[:])
 
-        window = held.tile([P, V], BF16, name="window")
-        table_blocks = table.rearrange("(c p) e -> p c e", p=P)
-        for g in range(V // (BLOCKS * P)):
-            loaded = rows.tile([P, BLOCKS, P], BF16, name="loaded")
-            queue = nc.sync if g % 2 == 0 else nc.scalar
-            queue.dma_start(loaded[:], table_blocks[:, g * BLOCKS : (g + 1) * BLOCKS, :])
-            turned = flip.tile([P, BLOCKS * P], BF16, name="turned")
-            for i in range(BLOCKS):
-                nc.tensor.transpose(turned[:, i * P : (i + 1) * P], loaded[:, i, :], identity[:])
-            columns = window[:, g * BLOCKS * P : (g + 1) * BLOCKS * P]
-            if g % 2 == 0:
-                nc.vector.tensor_copy(columns, turned[:])
-            else:
-                nc.scalar.copy(columns, turned[:])
+        table_loads = table.rearrange("(l c p) e -> l p c e", c=BLOCKS, p=P)
+        loaded = []
+        for l in range(loads):
+            loaded_l = rows.tile([P, BLOCKS, P], BF16, name="loaded")
+            queue = nc.sync if l % 2 == 0 else nc.scalar
+            queue.dma_start(loaded_l[:], table_loads[l])
+            loaded.append(loaded_l)
 
-        wh_sb = held.tile([P, D // P, M], BF16, name="wh_sb")
-        nc.sync.dma_start(wh_sb[:], wh.rearrange("(k p) m -> p k m", p=P))
-        h_sb = held.tile([P, D // P, P], BF16, name="h_sb")
-        nc.scalar.dma_start(h_sb[:], h.rearrange("(k p) r -> p k r", p=P))
-        posw_all = held.tile([P, P], F32, name="posw_all")
-        nc.sync.dma_start(posw_all[:], posw.rearrange("o r -> (o r)").partition_broadcast(P))
+        offsets = held.tile([P, N // 16], U16, name="offsets")
+        nc.sync.dma_start(offsets[:], offs)
+        w_sb = held.tile([P, M], BF16, name="w_sb")
+        nc.scalar.dma_start(w_sb[:], w)
 
         node = []
         for t in range(HALVES):
-            bias = held.tile([P, 1], F32, name=f"bias{t}")
-            nc.scalar.dma_start(bias[:], b[t * P : (t + 1) * P, :])
-            word_proj = proj.tile([P, P], F32, name="word_proj")
+            word_proj = banks.tile([P, P], F32, name="word_proj", tag="bank")
             for k in range(D // P):
                 nc.tensor.matmul(
                     word_proj[:], wh_sb[:, k, t * P : (t + 1) * P], h_sb[:, k, :],
@@ -72,14 +65,21 @@ def tile_typeenhancedgcndeepseek_kernel(tc, table, w, h, wh, posw, b, offs, out)
             weighted = work.tile([P, P], F32, name="weighted")
             nc.vector.tensor_tensor(weighted[:], word_proj[:], posw_all[:], MULT)
             node_t = held.tile([P, P], F32, name=f"node{t}")
-            nc.vector.tensor_scalar_add(node_t[:], weighted[:], bias[:])
+            nc.vector.tensor_scalar_add(node_t[:], weighted[:], bias[:, t : t + 1])
             node.append(node_t)
+
+        window = held.tile([P, V], BF16, name="window")
+        for l in range(loads):
+            turned = banks.tile([P, load_rows], BF16, name="turned", tag="bank")
+            for i in range(BLOCKS):
+                nc.tensor.transpose(turned[:, i * P : (i + 1) * P], loaded[l][:, i, :], identity[:])
+            nc.vector.tensor_copy(window[:, l * load_rows : (l + 1) * load_rows], turned[:])
 
         for piece in range(N // PIECE):
             piece_offsets = offsets[:, piece * (PIECE // 16) : (piece + 1) * (PIECE // 16)]
             summed = []
             for t in range(HALVES):
-                edge = pair.tile([P, PIECE], F32, name=f"edge{t}")
+                edge = banks.tile([P, PIECE], F32, name="edge", tag="bank")
                 nc.tensor.matmul(
                     edge[:], w_sb[:, t * P : (t + 1) * P], window[:].indirect(piece_offsets),
                     start=True, stop=True,

@@ -13,46 +13,57 @@ M = 256
 HALVES = M // P
 PIECE = 512
 WORDS = PIECE // Q
-BLOCKS = 4
+BLOCKS = 8
 
 FLOPS = 2 * P * M * N + 2 * D * M * P
 
 
 def tile_typeenhancedgcndeepseek_kernel(tc, table, w, h, wh, posw, b, offs, out):
     nc = tc.nc
-    load_rows = BLOCKS * P
-    loads = V // load_rows
+    group_rows = BLOCKS * P
+    loads = V // group_rows
     with (
         tc.tile_pool(name="held", bufs=1) as held,
         tc.tile_pool(name="rows", bufs=loads) as rows,
         tc.tile_pool(name="work", bufs=N // PIECE) as work,
         tc.psum_pool(name="banks", bufs=8) as banks,
     ):
-        h_sb = held.tile([P, D // P, P], BF16, name="h_sb")
-        nc.sync.dma_start(h_sb[:], h.rearrange("(k p) r -> p k r", p=P))
-        wh_sb = held.tile([P, D // P, M], BF16, name="wh_sb")
-        nc.scalar.dma_start(wh_sb[:], wh.rearrange("(k p) m -> p k m", p=P))
-        posw_all = held.tile([P, P], F32, name="posw_all")
-        nc.sync.dma_start(posw_all[:], posw.rearrange("o r -> (o r)").partition_broadcast(P))
-        bias = held.tile([P, HALVES], F32, name="bias")
-        with nc.allow_non_contiguous_dma(reason="256 single elements, one to a partition and layer"):
-            nc.scalar.dma_start(bias[:], b.rearrange("(t p) o -> p (t o)", p=P))
+        window = held.tile([P, V], BF16, name="window")
+        table_loads = table.rearrange("(l p c) e -> l p c e", c=BLOCKS, p=P)
+        loaded = []
+        for l in range(loads):
+            loaded_l = rows.tile([P, BLOCKS, P], BF16, name="loaded")
+            nc.sync.dma_start(loaded_l[:], table_loads[l])
+            loaded.append(loaded_l)
 
         identity = held.tile([P, P], BF16, name="identity")
         masks.make_identity(nc, identity[:])
 
-        table_loads = table.rearrange("(l c p) e -> l p c e", c=BLOCKS, p=P)
-        loaded = []
-        for l in range(loads):
-            loaded_l = rows.tile([P, BLOCKS, P], BF16, name="loaded")
-            queue = nc.sync if l % 2 == 0 else nc.scalar
-            queue.dma_start(loaded_l[:], table_loads[l])
-            loaded.append(loaded_l)
-
+        h_sb = held.tile([P, D // P, P], BF16, name="h_sb")
+        nc.sync.dma_start(h_sb[:], h.rearrange("(k p) r -> p k r", p=P))
+        wh_sb = held.tile([P, D // P, M], BF16, name="wh_sb")
+        nc.sync.dma_start(wh_sb[:], wh.rearrange("(k p) m -> p k m", p=P))
         offsets = held.tile([P, N // 16], U16, name="offsets")
         nc.sync.dma_start(offsets[:], offs)
         w_sb = held.tile([P, M], BF16, name="w_sb")
-        nc.scalar.dma_start(w_sb[:], w)
+        nc.sync.dma_start(w_sb[:], w)
+        posw_all = held.tile([P, P], F32, name="posw_all")
+        nc.sync.dma_start(posw_all[:], posw.rearrange("o r -> (o r)").partition_broadcast(P))
+        bias = held.tile([P, HALVES], F32, name="bias")
+        with nc.allow_non_contiguous_dma(reason="256 single elements, one to a partition and layer"):
+            nc.sync.dma_start(bias[:], b.rearrange("(t p) o -> p (t o)", p=P))
+
+        for l in range(loads):
+            turned = banks.tile([P, BLOCKS, P], BF16, name="turned", tag="bank")
+            for c in range(BLOCKS):
+                nc.tensor.transpose(turned[:, c, :], loaded[l][:, c, :], identity[:])
+            in_order = window[:, l * group_rows : (l + 1) * group_rows].rearrange(
+                "e (p c) -> e p c", c=BLOCKS
+            )
+            if l % 2 == 0:
+                nc.scalar.copy(in_order, turned[:].rearrange("e c p -> e p c"))
+            else:
+                nc.vector.tensor_copy(in_order, turned[:].rearrange("e c p -> e p c"))
 
         node = []
         for t in range(HALVES):
@@ -67,13 +78,6 @@ def tile_typeenhancedgcndeepseek_kernel(tc, table, w, h, wh, posw, b, offs, out)
             node_t = held.tile([P, P], F32, name=f"node{t}")
             nc.vector.tensor_scalar_add(node_t[:], weighted[:], bias[:, t : t + 1])
             node.append(node_t)
-
-        window = held.tile([P, V], BF16, name="window")
-        for l in range(loads):
-            turned = banks.tile([P, load_rows], BF16, name="turned", tag="bank")
-            for i in range(BLOCKS):
-                nc.tensor.transpose(turned[:, i * P : (i + 1) * P], loaded[l][:, i, :], identity[:])
-            nc.vector.tensor_copy(window[:, l * load_rows : (l + 1) * load_rows], turned[:])
 
         for piece in range(N // PIECE):
             piece_offsets = offsets[:, piece * (PIECE // 16) : (piece + 1) * (PIECE // 16)]

import concourse.masks as masks
import concourse.mybir as mybir

BF16, F32, U16 = mybir.dt.bfloat16, mybir.dt.float32, mybir.dt.uint16
ADD, MULT = mybir.AluOpType.add, mybir.AluOpType.mult

P = 128
V = 4096
N = 2048
Q = 16
D = 256
M = 256
HALVES = M // P
PIECE = 512
WORDS = PIECE // Q
BLOCKS = 8

FLOPS = 2 * P * M * N + 2 * D * M * P


def tile_typeenhancedgcndeepseek_kernel(tc, table, w, h, wh, posw, b, offs, out):
    nc = tc.nc
    group_rows = BLOCKS * P
    loads = V // group_rows
    with (
        tc.tile_pool(name="held", bufs=1) as held,
        tc.tile_pool(name="rows", bufs=loads) as rows,
        tc.tile_pool(name="work", bufs=N // PIECE) as work,
        tc.psum_pool(name="banks", bufs=8) as banks,
    ):
        window = held.tile([P, V], BF16, name="window")
        table_loads = table.rearrange("(l p c) e -> l p c e", c=BLOCKS, p=P)
        loaded = []
        for l in range(loads):
            loaded_l = rows.tile([P, BLOCKS, P], BF16, name="loaded")
            nc.sync.dma_start(loaded_l[:], table_loads[l])
            loaded.append(loaded_l)

        identity = held.tile([P, P], BF16, name="identity")
        masks.make_identity(nc, identity[:])

        h_sb = held.tile([P, D // P, P], BF16, name="h_sb")
        nc.sync.dma_start(h_sb[:], h.rearrange("(k p) r -> p k r", p=P))
        wh_sb = held.tile([P, D // P, M], BF16, name="wh_sb")
        nc.sync.dma_start(wh_sb[:], wh.rearrange("(k p) m -> p k m", p=P))
        offsets = held.tile([P, N // 16], U16, name="offsets")
        nc.sync.dma_start(offsets[:], offs)
        w_sb = held.tile([P, M], BF16, name="w_sb")
        nc.sync.dma_start(w_sb[:], w)
        posw_all = held.tile([P, P], F32, name="posw_all")
        nc.sync.dma_start(posw_all[:], posw.rearrange("o r -> (o r)").partition_broadcast(P))
        bias = held.tile([P, HALVES], F32, name="bias")
        with nc.allow_non_contiguous_dma(reason="256 single elements, one to a partition and layer"):
            nc.sync.dma_start(bias[:], b.rearrange("(t p) o -> p (t o)", p=P))

        for l in range(loads):
            turned = banks.tile([P, BLOCKS, P], BF16, name="turned", tag="bank")
            for c in range(BLOCKS):
                nc.tensor.transpose(turned[:, c, :], loaded[l][:, c, :], identity[:])
            in_order = window[:, l * group_rows : (l + 1) * group_rows].rearrange(
                "e (p c) -> e p c", c=BLOCKS
            )
            if l % 2 == 0:
                nc.scalar.copy(in_order, turned[:].rearrange("e c p -> e p c"))
            else:
                nc.vector.tensor_copy(in_order, turned[:].rearrange("e c p -> e p c"))

        node = []
        for t in range(HALVES):
            word_proj = banks.tile([P, P], F32, name="word_proj", tag="bank")
            for k in range(D // P):
                nc.tensor.matmul(
                    word_proj[:], wh_sb[:, k, t * P : (t + 1) * P], h_sb[:, k, :],
                    start=(k == 0), stop=(k == D // P - 1),
                )
            weighted = work.tile([P, P], F32, name="weighted")
            nc.vector.tensor_tensor(weighted[:], word_proj[:], posw_all[:], MULT)
            node_t = held.tile([P, P], F32, name=f"node{t}")
            nc.vector.tensor_scalar_add(node_t[:], weighted[:], bias[:, t : t + 1])
            node.append(node_t)

        for piece in range(N // PIECE):
            piece_offsets = offsets[:, piece * (PIECE // 16) : (piece + 1) * (PIECE // 16)]
            summed = []
            for t in range(HALVES):
                edge = banks.tile([P, PIECE], F32, name="edge", tag="bank")
                nc.tensor.matmul(
                    edge[:], w_sb[:, t * P : (t + 1) * P], window[:].indirect(piece_offsets),
                    start=True, stop=True,
                )
                p_t = work.tile([P, PIECE], F32, name=f"p{t}")
                node_of_pair = (
                    node[t][:, piece * WORDS : (piece + 1) * WORDS]
                    .unsqueeze(2)
                    .to_broadcast([P, WORDS, Q])
                )
                nc.vector.tensor_tensor(
                    p_t[:].rearrange("m (r q) -> m r q", q=Q),
                    edge[:].rearrange("m (r q) -> m r q", q=Q),
                    node_of_pair,
                    ADD,
                )
                summed.append(p_t)
            product = work.tile([P, PIECE], F32, name="product")
            multiplier = nc.gpsimd if piece < N // PIECE - 1 else nc.vector
            multiplier.tensor_tensor(product[:], summed[0][:], summed[1][:], MULT)
            nc.sync.dma_start(out[:, piece * PIECE : (piece + 1) * PIECE], product[:])
